import numpy as np
import ml_dtypes


def mxq(x, axis, fmt="e4m3"):
    dtype, down = {"e4m3": (ml_dtypes.float8_e4m3fn, 7), "e5m2": (ml_dtypes.float8_e5m2, 14)}[fmt]
    v = np.moveaxis(np.asarray(x, np.float32).astype(ml_dtypes.bfloat16).astype(np.float64), axis, -1)
    blocks = v.reshape(v.shape[:-1] + (-1, 32))
    amax = np.abs(blocks).max(-1, keepdims=True)
    byte = np.maximum(np.where(amax > 0, np.frexp(amax)[1] - 1 + 127, 0) - down, 1)
    scale = np.exp2(byte - 127.0)
    codes = (blocks / scale).astype(np.float32).astype(dtype).astype(np.float64)
    return np.moveaxis((codes * scale).reshape(v.shape), -1, axis)


WIDE = False


def mx_kscale(k):
    if not WIDE:
        return np.ones(k)
    levels = np.array([10, -10, 5, -5, 0])
    a = np.random.permutation(np.resize(levels, k // 512 * 4)).reshape(k // 512, 4)
    idx = np.arange(k)
    return np.exp2(a[idx // 512, idx % 128 // 32])


BF16 = ml_dtypes.bfloat16


def bf(x):
    return np.asarray(x, np.float32).astype(BF16)


def f64(x):
    return np.asarray(x).astype(np.float64)


E2M1 = np.array([0.0, 0.5, 1.0, 1.5, 2.0, 3.0, 4.0, 6.0, -0.0, -0.5, -1.0, -1.5, -2.0, -3.0, -4.0, -6.0])


def pack_weight(w, fmt):
    k, n = w.shape
    w = f64(bf(w)).reshape(k // 32, 32, n)
    amax = np.abs(w).max(1)
    if fmt == "e4m3":
        byte = np.frexp(amax)[1] - 1 + 127 - 7
    else:
        mant, ex = np.frexp(amax / 6.0)
        byte = np.where(mant > 0.5, ex, ex - 1) + 127
    byte = np.clip(np.where(amax > 0, byte, 1), 1, 254)
    scaled = (w * np.exp2(127.0 - byte)[:, None, :]).reshape(k, n).astype(np.float32)
    by_word = np.ascontiguousarray(scaled.reshape(k // 512, 128, 4, n).transpose(0, 1, 3, 2))
    if fmt == "e4m3":
        words = by_word.astype(ml_dtypes.float8_e4m3fn).view(np.uint8)
    else:
        c = by_word.astype(ml_dtypes.float4_e2m1fn).view(np.uint8) & 0xF
        words = c[..., 0::2] | (c[..., 1::2] << 4)
    return np.ascontiguousarray(words), np.ascontiguousarray(byte.astype(np.uint8).reshape(k // 512, 16, n))


def unpack_weight(words, scales, fmt):
    g, p, n, _ = words.shape
    if fmt == "e4m3":
        vals = np.ascontiguousarray(words).view(ml_dtypes.float8_e4m3fn).astype(np.float64)
    else:
        nib = np.empty((g, p, n, 4), np.uint8)
        nib[..., 0::2] = words & 0xF
        nib[..., 1::2] = words >> 4
        vals = E2M1[nib]
    vals = vals * np.repeat(np.exp2(scales.astype(np.float64) - 127.0), 8, axis=1)[..., None]
    return vals.transpose(0, 1, 3, 2).reshape(g * 512, n)


def pack4(w):
    words, scales = pack_weight(w, "e2m1")
    return words.reshape(words.shape[0], 128, -1), scales


def unpack4(words, scales):
    return unpack_weight(words.reshape(words.shape[0], 128, -1, 2), scales, "e2m1")


T, D_IN, D_OUT = 128, 4096, 8192


def setup_inputs():
    s = mx_kscale(D_IN)
    x = bf(np.random.standard_normal((T, D_IN)) * s)
    w = np.random.standard_normal((D_IN, D_OUT)) / 64.0 / s[:, None]
    w_words, w_scales = pack4(w)
    bias = bf(np.random.standard_normal(D_OUT) * 0.5)
    return {"x": x, "w_words": w_words, "w_scales": w_scales, "bias": bias}


def reference(x, w_words, w_scales, bias):
    w = unpack4(w_words, w_scales)
    return (mxq(f64(x), 1, "e4m3") @ w) + f64(bias)[None, :]

@@ -1,0 +1,162 @@
+from contextlib import ExitStack
+
+import concourse.mybir as mybir
+from concourse.masks import make_identity
+
+FLOPS = 2 * 128 * 4096 * 8192
+
+F32 = mybir.dt.float32
+BF16 = mybir.dt.bfloat16
+I32 = mybir.dt.int32
+U8 = mybir.dt.uint8
+U32 = mybir.dt.uint32
+FP8X4 = mybir.dt.float8_e4m3fn_x4
+FP4X4 = mybir.dt.float4_e2m1fn_x4
+
+P = 128
+G = 8
+N = 8192
+BANK = 512
+HALF = 4096
+NB = HALF // BANK
+W_BUFS = 10
+RPD = 2
+MEMSET_G = 2
+
+
+def tile_linearfp8_kernel(tc, x, w_words, w_scales, bias, out):
+    nc = tc.nc
+    with ExitStack() as ctx:
+        keep = ctx.enter_context(tc.tile_pool(name="keep", bufs=1))
+        wpool = ctx.enter_context(tc.tile_pool(name="wpool", bufs=W_BUFS))
+        psum = ctx.enter_context(tc.psum_pool(name="psum", bufs=1))
+        ctx.enter_context(tc.manual_schedule())
+
+        ident_f32 = keep.tile([P, P], F32, name="ident_f32")
+        ident_bf = keep.tile([P, P], BF16, name="ident_bf")
+        bias_rows = keep.tile([P, BANK], BF16, name="bias_rows")
+        bias_bc = keep.tile([P, N], BF16, name="bias_bc")
+        x_sb = keep.tile([P, G * 512], BF16, name="x_sb")
+        grouped = keep.tile([P, G * 512], BF16, name="grouped", align_bytes=64)
+        x_codes = keep.tile([P, G * P], U32, name="x_codes", align_bytes=64)
+        x_scales = keep.tile([P, G * P], U8, name="x_scales", align_bytes=64)
+        planes = [
+            keep.tile([P, G, HALF], U8, name="plane%d" % h, align_bytes=64) for h in range(2)
+        ]
+        out_sb = keep.tile([P, N], F32, name="out_sb")
+
+        make_identity(nc, ident_f32[:])
+        make_identity(nc, ident_bf[:])
+        nc.vector.memset(bias_rows[:], 0.0)
+
+        nc.sync.dma_start(out=x_sb[:], in_=x)
+        nc.sync.dma_start(
+            out=bias_rows[0 : N // BANK, :], in_=bias.rearrange("(j n) -> j n", n=BANK)
+        )
+
+        for h in range(2):
+            for g0 in range(0, G, MEMSET_G):
+                nc.vector.memset(
+                    planes[h][:, g0 : g0 + MEMSET_G, :]
+                    .rearrange("p g n -> p (g n)")
+                    .bitcast(I32),
+                    0,
+                )
+
+        def load_scales(h):
+            for g0 in range(0, G, RPD):
+                for b in range(2):
+                    for r in range(4):
+                        nc.sync.dma_start(
+                            out=planes[h][32 * b + r : P : 64, g0 : g0 + RPD, :].bitcast(I32),
+                            in_=w_scales[
+                                g0 : g0 + RPD, 4 * b + r : 16 : 8, HALF * h : HALF * (h + 1)
+                            ]
+                            .rearrange("g q n -> q g n")
+                            .bitcast(I32),
+                        )
+
+        slabs = {}
+
+        def load_slab(s):
+            h, g = divmod(s, G)
+            wt = wpool.tile([P, 2 * HALF], U8, name="wt", tag="wt", align_bytes=64)
+            nc.sync.dma_start(
+                out=wt[:].bitcast(I32),
+                in_=w_words[g, :, 2 * HALF * h : 2 * HALF * (h + 1)].bitcast(I32),
+            )
+            slabs[s] = wt
+
+        load_scales(0)
+        for s in range(G):
+            load_slab(s)
+        load_scales(1)
+        for s in range(G, W_BUFS):
+            load_slab(s)
+
+        x32 = x_sb[:].bitcast(F32)
+        grouped32 = grouped[:].bitcast(F32).rearrange("p (g r u) -> p g r u", r=P, u=2)
+        for bk in range(G // 2):
+            xt = psum.tile([P, 2, 2, P], F32, name="xt%d" % bk, tag="bank%d" % bk)
+            for gg in range(2):
+                g = 2 * bk + gg
+                for u in range(2):
+                    nc.tensor.transpose(
+                        xt[:, gg, u, :], x32[:, 256 * g + u : 256 * (g + 1) : 2], ident_f32[:]
+                    )
+            nc.scalar.copy(
+                out=grouped32[:, 2 * bk : 2 * bk + 2, :, :],
+                in_=xt[:].rearrange("p g u r -> p g r u"),
+            )
+        nc.vector.quantize_mx(
+            out=x_codes[:].bitcast(FP8X4), scales=x_scales[:], in_=grouped[:]
+        )
+
+        for j in range(N // BANK):
+            bk = (4 + j) % 8
+            bp = psum.tile([P, BANK], F32, name="bp%d" % j, tag="bank%d" % bk)
+            nc.tensor.matmul(
+                out=bp[:],
+                lhsT=ident_bf[:, j : j + 1].to_broadcast([P, P]),
+                rhs=bias_rows[:],
+                start=True,
+                stop=True,
+            )
+            dst = bias_bc[:, BANK * j : BANK * (j + 1)]
+            if j % 2 == 0:
+                nc.scalar.copy(out=dst, in_=bp[:])
+            else:
+                nc.vector.tensor_copy(out=dst, in_=bp[:])
+
+        for h in range(2):
+            accs = [
+                psum.tile([P, BANK], F32, name="acc%d_%d" % (h, j), tag="bank%d" % j)
+                for j in range(NB)
+            ]
+            for g in range(G):
+                s = G * h + g
+                wt = slabs[s]
+                for j in range(NB):
+                    nc.tensor.matmul_mx(
+                        out=accs[j][:],
+                        lhsT=x_codes[:, P * g : P * (g + 1)].bitcast(FP8X4),
+                        lhsT_scale=x_scales[:, P * g : P * (g + 1)],
+                        rhs=wt[:, 2 * BANK * j : 2 * BANK * (j + 1)].bitcast(FP4X4),
+                        rhs_scale=planes[h][:, g, BANK * j : BANK * (j + 1)],
+                        start=(g == 0),
+                        stop=(g == G - 1),
+                    )
+                    if g == G - 1:
+                        c0 = HALF * h + BANK * j
+                        nc.vector.tensor_tensor(
+                            out=out_sb[:, c0 : c0 + BANK],
+                            in0=accs[j][:],
+                            in1=bias_bc[:, c0 : c0 + BANK],
+                            op=mybir.AluOpType.add,
+                        )
+                if s + W_BUFS < 2 * G:
+                    load_slab(s + W_BUFS)
+
+        nc.sync.dma_start(out=out[:, 0:HALF], in_=out_sb[:, 0:HALF])
+        for c0 in range(HALF, N, 2 * BANK):
+            nc.sync.dma_start(out=out[:, c0 : c0 + 2 * BANK], in_=out_sb[:, c0 : c0 + 2 * BANK])

@@ -23,6 +23,13 @@ W_BUFS = 10
 RPD = 2
 MEMSET_G = 2
 
+UNITS = [(s, 0, NB) for s in range(2 * G - 2)] + [
+    (2 * G - 2, 0, NB // 2),
+    (2 * G - 1, 0, NB // 2),
+    (2 * G - 2, NB // 2, NB),
+    (2 * G - 1, NB // 2, NB),
+]
+
 
 def tile_linearfp8_kernel(tc, x, w_words, w_scales, bias, out):
     nc = tc.nc
@@ -77,22 +84,28 @@ def tile_linearfp8_kernel(tc, x, w_words, w_scales, bias, out):
                         )
 
         slabs = {}
+        finished = []
+        state = {"next": 0}
 
-        def load_slab(s):
-            h, g = divmod(s, G)
-            wt = wpool.tile([P, 2 * HALF], U8, name="wt", tag="wt", align_bytes=64)
-            nc.sync.dma_start(
-                out=wt[:].bitcast(I32),
-                in_=w_words[g, :, 2 * HALF * h : 2 * HALF * (h + 1)].bitcast(I32),
-            )
-            slabs[s] = wt
+        def load_units():
+            while state["next"] < len(UNITS):
+                s, j0, j1 = UNITS[state["next"]]
+                h, g = divmod(s, G)
+                if s not in slabs:
+                    if len(slabs) - len(finished) >= W_BUFS:
+                        return
+                    if g == 0:
+                        load_scales(h)
+                    slabs[s] = wpool.tile([P, 2 * HALF], U8, name="wt", tag="wt", align_bytes=64)
+                b0 = 2 * BANK * j0
+                b1 = 2 * BANK * j1
+                nc.sync.dma_start(
+                    out=slabs[s][:, b0:b1].bitcast(I32),
+                    in_=w_words[g, :, 2 * HALF * h + b0 : 2 * HALF * h + b1].bitcast(I32),
+                )
+                state["next"] += 1
 
-        load_scales(0)
-        for s in range(G):
-            load_slab(s)
-        load_scales(1)
-        for s in range(G, W_BUFS):
-            load_slab(s)
+        load_units()
 
         x32 = x_sb[:].bitcast(F32)
         grouped32 = grouped[:].bitcast(F32).rearrange("p (g r u) -> p g r u", r=P, u=2)
@@ -128,35 +141,42 @@ def tile_linearfp8_kernel(tc, x, w_words, w_scales, bias, out):
             else:
                 nc.vector.tensor_copy(out=dst, in_=bp[:])
 
-        for h in range(2):
-            accs = [
-                psum.tile([P, BANK], F32, name="acc%d_%d" % (h, j), tag="bank%d" % j)
-                for j in range(NB)
-            ]
-            for g in range(G):
-                s = G * h + g
-                wt = slabs[s]
-                for j in range(NB):
-                    nc.tensor.matmul_mx(
-                        out=accs[j][:],
-                        lhsT=x_codes[:, P * g : P * (g + 1)].bitcast(FP8X4),
-                        lhsT_scale=x_scales[:, P * g : P * (g + 1)],
-                        rhs=wt[:, 2 * BANK * j : 2 * BANK * (j + 1)].bitcast(FP4X4),
-                        rhs_scale=planes[h][:, g, BANK * j : BANK * (j + 1)],
-                        start=(g == 0),
-                        stop=(g == G - 1),
-                    )
-                    if g == G - 1:
-                        c0 = HALF * h + BANK * j
-                        nc.vector.tensor_tensor(
-                            out=out_sb[:, c0 : c0 + BANK],
-                            in0=accs[j][:],
-                            in1=bias_bc[:, c0 : c0 + BANK],
-                            op=mybir.AluOpType.add,
-                        )
-                if s + W_BUFS < 2 * G:
-                    load_slab(s + W_BUFS)
+        def store(c0, c1):
+            nc.sync.dma_start(out=out[:, c0:c1], in_=out_sb[:, c0:c1])
 
-        nc.sync.dma_start(out=out[:, 0:HALF], in_=out_sb[:, 0:HALF])
-        for c0 in range(HALF, N, 2 * BANK):
-            nc.sync.dma_start(out=out[:, c0 : c0 + 2 * BANK], in_=out_sb[:, c0 : c0 + 2 * BANK])
+        accs = {}
+        for u, (s, j0, j1) in enumerate(UNITS):
+            h, g = divmod(s, G)
+            if g == 0:
+                accs[h] = [
+                    psum.tile([P, BANK], F32, name="acc%d_%d" % (h, j), tag="bank%d" % j)
+                    for j in range(NB)
+                ]
+            for j in range(j0, j1):
+                nc.tensor.matmul_mx(
+                    out=accs[h][j][:],
+                    lhsT=x_codes[:, P * g : P * (g + 1)].bitcast(FP8X4),
+                    lhsT_scale=x_scales[:, P * g : P * (g + 1)],
+                    rhs=slabs[s][:, 2 * BANK * j : 2 * BANK * (j + 1)].bitcast(FP4X4),
+                    rhs_scale=planes[h][:, g, BANK * j : BANK * (j + 1)],
+                    start=(g == 0),
+                    stop=(g == G - 1),
+                )
+                if g == G - 1:
+                    c0 = HALF * h + BANK * j
+                    nc.vector.tensor_tensor(
+                        out=out_sb[:, c0 : c0 + BANK],
+                        in0=accs[h][j][:],
+                        in1=bias_bc[:, c0 : c0 + BANK],
+                        op=mybir.AluOpType.add,
+                    )
+            if all(v[0] != s for v in UNITS[u + 1 :]):
+                finished.append(s)
+                load_units()
+            if s == G - 1:
+                store(0, HALF)
+            if s == 2 * G - 1 and j1 == NB // 2:
+                store(HALF, HALF + 4 * BANK)
+            if s == 2 * G - 1 and j1 == NB:
+                store(HALF + 4 * BANK, HALF + 6 * BANK)
+                store(HALF + 6 * BANK, N)

@@ -20,8 +20,7 @@ BANK = 512
 HALF = 4096
 NB = HALF // BANK
 W_BUFS = 10
-RPD = 2
-MEMSET_G = 2
+SCALE_RUNS = [(0, 1), (1, 3), (4, 3), (7, 1)]
 
 UNITS = [(s, 0, NB) for s in range(2 * G - 2)] + [
     (2 * G - 2, 0, NB // 2),
@@ -47,9 +46,7 @@ def tile_linearfp8_kernel(tc, x, w_words, w_scales, bias, out):
         grouped = keep.tile([P, G * 512], BF16, name="grouped", align_bytes=64)
         x_codes = keep.tile([P, G * P], U32, name="x_codes", align_bytes=64)
         x_scales = keep.tile([P, G * P], U8, name="x_scales", align_bytes=64)
-        planes = [
-            keep.tile([P, G, HALF], U8, name="plane%d" % h, align_bytes=64) for h in range(2)
-        ]
+        planes = keep.tile([P, G, N], U8, name="planes", align_bytes=64)
         out_sb = keep.tile([P, N], F32, name="out_sb")
 
         make_identity(nc, ident_f32[:])
@@ -61,27 +58,18 @@ def tile_linearfp8_kernel(tc, x, w_words, w_scales, bias, out):
             out=bias_rows[0 : N // BANK, :], in_=bias.rearrange("(j n) -> j n", n=BANK)
         )
 
-        for h in range(2):
-            for g0 in range(0, G, MEMSET_G):
-                nc.vector.memset(
-                    planes[h][:, g0 : g0 + MEMSET_G, :]
-                    .rearrange("p g n -> p (g n)")
-                    .bitcast(I32),
-                    0,
-                )
+        for g in range(G):
+            nc.vector.memset(planes[:, g, :].bitcast(I32), 0)
 
-        def load_scales(h):
-            for g0 in range(0, G, RPD):
-                for b in range(2):
-                    for r in range(4):
-                        nc.sync.dma_start(
-                            out=planes[h][32 * b + r : P : 64, g0 : g0 + RPD, :].bitcast(I32),
-                            in_=w_scales[
-                                g0 : g0 + RPD, 4 * b + r : 16 : 8, HALF * h : HALF * (h + 1)
-                            ]
-                            .rearrange("g q n -> q g n")
-                            .bitcast(I32),
-                        )
+        for g0, ng in SCALE_RUNS:
+            for b in range(2):
+                for r in range(4):
+                    nc.sync.dma_start(
+                        out=planes[32 * b + r : P : 64, g0 : g0 + ng, :].bitcast(I32),
+                        in_=w_scales[g0 : g0 + ng, 4 * b + r : 16 : 8, :]
+                        .rearrange("g q n -> q g n")
+                        .bitcast(I32),
+                    )
 
         slabs = {}
         finished = []
@@ -94,8 +82,6 @@ def tile_linearfp8_kernel(tc, x, w_words, w_scales, bias, out):
                 if s not in slabs:
                     if len(slabs) - len(finished) >= W_BUFS:
                         return
-                    if g == 0:
-                        load_scales(h)
                     slabs[s] = wpool.tile([P, 2 * HALF], U8, name="wt", tag="wt", align_bytes=64)
                 b0 = 2 * BANK * j0
                 b1 = 2 * BANK * j1
@@ -158,22 +144,32 @@ def tile_linearfp8_kernel(tc, x, w_words, w_scales, bias, out):
                     lhsT=x_codes[:, P * g : P * (g + 1)].bitcast(FP8X4),
                     lhsT_scale=x_scales[:, P * g : P * (g + 1)],
                     rhs=slabs[s][:, 2 * BANK * j : 2 * BANK * (j + 1)].bitcast(FP4X4),
-                    rhs_scale=planes[h][:, g, BANK * j : BANK * (j + 1)],
+                    rhs_scale=planes[:, g, HALF * h + BANK * j : HALF * h + BANK * (j + 1)],
                     start=(g == 0),
                     stop=(g == G - 1),
                 )
                 if g == G - 1:
                     c0 = HALF * h + BANK * j
-                    nc.vector.tensor_tensor(
-                        out=out_sb[:, c0 : c0 + BANK],
-                        in0=accs[h][j][:],
-                        in1=bias_bc[:, c0 : c0 + BANK],
-                        op=mybir.AluOpType.add,
-                    )
+                    if h == 0 and j % 2 == 1:
+                        nc.scalar.copy(out=out_sb[:, c0 : c0 + BANK], in_=accs[h][j][:])
+                    else:
+                        nc.vector.tensor_tensor(
+                            out=out_sb[:, c0 : c0 + BANK],
+                            in0=accs[h][j][:],
+                            in1=bias_bc[:, c0 : c0 + BANK],
+                            op=mybir.AluOpType.add,
+                        )
             if all(v[0] != s for v in UNITS[u + 1 :]):
                 finished.append(s)
                 load_units()
             if s == G - 1:
+                for j in range(1, NB, 2):
+                    nc.vector.tensor_tensor(
+                        out=out_sb[:, BANK * j : BANK * (j + 1)],
+                        in0=out_sb[:, BANK * j : BANK * (j + 1)],
+                        in1=bias_bc[:, BANK * j : BANK * (j + 1)],
+                        op=mybir.AluOpType.add,
+                    )
                 store(0, HALF)
             if s == 2 * G - 1 and j1 == NB // 2:
                 store(HALF, HALF + 4 * BANK)

@@ -20,7 +20,7 @@ BANK = 512
 HALF = 4096
 NB = HALF // BANK
 W_BUFS = 10
-SCALE_RUNS = [(0, 1), (1, 3), (4, 3), (7, 1)]
+SCALE_RUNS = [(0, 1), (1, 2), (3, 4), (7, 1)]
 
 UNITS = [(s, 0, NB) for s in range(2 * G - 2)] + [
     (2 * G - 2, 0, NB // 2),

from contextlib import ExitStack

import concourse.mybir as mybir
from concourse.masks import make_identity

FLOPS = 2 * 128 * 4096 * 8192

F32 = mybir.dt.float32
BF16 = mybir.dt.bfloat16
I32 = mybir.dt.int32
U8 = mybir.dt.uint8
U32 = mybir.dt.uint32
FP8X4 = mybir.dt.float8_e4m3fn_x4
FP4X4 = mybir.dt.float4_e2m1fn_x4

P = 128
G = 8
N = 8192
BANK = 512
HALF = 4096
NB = HALF // BANK
W_BUFS = 10
SCALE_RUNS = [(0, 1), (1, 2), (3, 4), (7, 1)]

UNITS = [(s, 0, NB) for s in range(2 * G - 2)] + [
    (2 * G - 2, 0, NB // 2),
    (2 * G - 1, 0, NB // 2),
    (2 * G - 2, NB // 2, NB),
    (2 * G - 1, NB // 2, NB),
]


def tile_linearfp8_kernel(tc, x, w_words, w_scales, bias, out):
    nc = tc.nc
    with ExitStack() as ctx:
        keep = ctx.enter_context(tc.tile_pool(name="keep", bufs=1))
        wpool = ctx.enter_context(tc.tile_pool(name="wpool", bufs=W_BUFS))
        psum = ctx.enter_context(tc.psum_pool(name="psum", bufs=1))
        ctx.enter_context(tc.manual_schedule())

        ident_f32 = keep.tile([P, P], F32, name="ident_f32")
        ident_bf = keep.tile([P, P], BF16, name="ident_bf")
        bias_rows = keep.tile([P, BANK], BF16, name="bias_rows")
        bias_bc = keep.tile([P, N], BF16, name="bias_bc")
        x_sb = keep.tile([P, G * 512], BF16, name="x_sb")
        grouped = keep.tile([P, G * 512], BF16, name="grouped", align_bytes=64)
        x_codes = keep.tile([P, G * P], U32, name="x_codes", align_bytes=64)
        x_scales = keep.tile([P, G * P], U8, name="x_scales", align_bytes=64)
        planes = keep.tile([P, G, N], U8, name="planes", align_bytes=64)
        out_sb = keep.tile([P, N], F32, name="out_sb")

        make_identity(nc, ident_f32[:])
        make_identity(nc, ident_bf[:])
        nc.vector.memset(bias_rows[:], 0.0)

        nc.sync.dma_start(out=x_sb[:], in_=x)
        nc.sync.dma_start(
            out=bias_rows[0 : N // BANK, :], in_=bias.rearrange("(j n) -> j n", n=BANK)
        )

        for g in range(G):
            nc.vector.memset(planes[:, g, :].bitcast(I32), 0)

        for g0, ng in SCALE_RUNS:
            for b in range(2):
                for r in range(4):
                    nc.sync.dma_start(
                        out=planes[32 * b + r : P : 64, g0 : g0 + ng, :].bitcast(I32),
                        in_=w_scales[g0 : g0 + ng, 4 * b + r : 16 : 8, :]
                        .rearrange("g q n -> q g n")
                        .bitcast(I32),
                    )

        slabs = {}
        finished = []
        state = {"next": 0}

        def load_units():
            while state["next"] < len(UNITS):
                s, j0, j1 = UNITS[state["next"]]
                h, g = divmod(s, G)
                if s not in slabs:
                    if len(slabs) - len(finished) >= W_BUFS:
                        return
                    slabs[s] = wpool.tile([P, 2 * HALF], U8, name="wt", tag="wt", align_bytes=64)
                b0 = 2 * BANK * j0
                b1 = 2 * BANK * j1
                nc.sync.dma_start(
                    out=slabs[s][:, b0:b1].bitcast(I32),
                    in_=w_words[g, :, 2 * HALF * h + b0 : 2 * HALF * h + b1].bitcast(I32),
                )
                state["next"] += 1

        load_units()

        x32 = x_sb[:].bitcast(F32)
        grouped32 = grouped[:].bitcast(F32).rearrange("p (g r u) -> p g r u", r=P, u=2)
        for bk in range(G // 2):
            xt = psum.tile([P, 2, 2, P], F32, name="xt%d" % bk, tag="bank%d" % bk)
            for gg in range(2):
                g = 2 * bk + gg
                for u in range(2):
                    nc.tensor.transpose(
                        xt[:, gg, u, :], x32[:, 256 * g + u : 256 * (g + 1) : 2], ident_f32[:]
                    )
            nc.scalar.copy(
                out=grouped32[:, 2 * bk : 2 * bk + 2, :, :],
                in_=xt[:].rearrange("p g u r -> p g r u"),
            )
        nc.vector.quantize_mx(
            out=x_codes[:].bitcast(FP8X4), scales=x_scales[:], in_=grouped[:]
        )

        for j in range(N // BANK):
            bk = (4 + j) % 8
            bp = psum.tile([P, BANK], F32, name="bp%d" % j, tag="bank%d" % bk)
            nc.tensor.matmul(
                out=bp[:],
                lhsT=ident_bf[:, j : j + 1].to_broadcast([P, P]),
                rhs=bias_rows[:],
                start=True,
                stop=True,
            )
            dst = bias_bc[:, BANK * j : BANK * (j + 1)]
            if j % 2 == 0:
                nc.scalar.copy(out=dst, in_=bp[:])
            else:
                nc.vector.tensor_copy(out=dst, in_=bp[:])

        def store(c0, c1):
            nc.sync.dma_start(out=out[:, c0:c1], in_=out_sb[:, c0:c1])

        accs = {}
        for u, (s, j0, j1) in enumerate(UNITS):
            h, g = divmod(s, G)
            if g == 0:
                accs[h] = [
                    psum.tile([P, BANK], F32, name="acc%d_%d" % (h, j), tag="bank%d" % j)
                    for j in range(NB)
                ]
            for j in range(j0, j1):
                nc.tensor.matmul_mx(
                    out=accs[h][j][:],
                    lhsT=x_codes[:, P * g : P * (g + 1)].bitcast(FP8X4),
                    lhsT_scale=x_scales[:, P * g : P * (g + 1)],
                    rhs=slabs[s][:, 2 * BANK * j : 2 * BANK * (j + 1)].bitcast(FP4X4),
                    rhs_scale=planes[:, g, HALF * h + BANK * j : HALF * h + BANK * (j + 1)],
                    start=(g == 0),
                    stop=(g == G - 1),
                )
                if g == G - 1:
                    c0 = HALF * h + BANK * j
                    if h == 0 and j % 2 == 1:
                        nc.scalar.copy(out=out_sb[:, c0 : c0 + BANK], in_=accs[h][j][:])
                    else:
                        nc.vector.tensor_tensor(
                            out=out_sb[:, c0 : c0 + BANK],
                            in0=accs[h][j][:],
                            in1=bias_bc[:, c0 : c0 + BANK],
                            op=mybir.AluOpType.add,
                        )
            if all(v[0] != s for v in UNITS[u + 1 :]):
                finished.append(s)
                load_units()
            if s == G - 1:
                for j in range(1, NB, 2):
                    nc.vector.tensor_tensor(
                        out=out_sb[:, BANK * j : BANK * (j + 1)],
                        in0=out_sb[:, BANK * j : BANK * (j + 1)],
                        in1=bias_bc[:, BANK * j : BANK * (j + 1)],
                        op=mybir.AluOpType.add,
                    )
                store(0, HALF)
            if s == 2 * G - 1 and j1 == NB // 2:
                store(HALF, HALF + 4 * BANK)
            if s == 2 * G - 1 and j1 == NB:
                store(HALF + 4 * BANK, HALF + 6 * BANK)
                store(HALF + 6 * BANK, N)
